import numpy as np
import ml_dtypes


def mxq(x, axis, fmt="e4m3"):
    dtype, down = {"e4m3": (ml_dtypes.float8_e4m3fn, 7), "e5m2": (ml_dtypes.float8_e5m2, 14)}[fmt]
    v = np.moveaxis(np.asarray(x, np.float32).astype(ml_dtypes.bfloat16).astype(np.float64), axis, -1)
    blocks = v.reshape(v.shape[:-1] + (-1, 32))
    amax = np.abs(blocks).max(-1, keepdims=True)
    byte = np.maximum(np.where(amax > 0, np.frexp(amax)[1] - 1 + 127, 0) - down, 1)
    scale = np.exp2(byte - 127.0)
    codes = (blocks / scale).astype(np.float32).astype(dtype).astype(np.float64)
    return np.moveaxis((codes * scale).reshape(v.shape), -1, axis)


WIDE = False


def mx_kscale(k):
    if not WIDE:
        return np.ones(k)
    levels = np.array([10, -10, 5, -5, 0])
    a = np.random.permutation(np.resize(levels, k // 512 * 4)).reshape(k // 512, 4)
    idx = np.arange(k)
    return np.exp2(a[idx // 512, idx % 128 // 32])


BF16 = ml_dtypes.bfloat16


def bf(x):
    return np.asarray(x, np.float32).astype(BF16)


def f64(x):
    return np.asarray(x).astype(np.float64)


B, I, O, DEG = 8192, 512, 128, 5
LN_EPS = 1e-5


def gottlieb_basis(x, alpha, degree):
    a = alpha[0]
    basis = [np.ones_like(x)]
    if degree >= 1:
        basis.append(2.0 * a * x)
    for n in range(2, degree + 1):
        basis.append(2.0 * (a + (n - 1)) * x * basis[-1] - (a + (2 * n - 2)) * basis[-2])
    return np.stack(basis, axis=0)


def setup_inputs():
    s = mx_kscale(I)
    u = s / s.max()
    p = u / (1.0 + np.exp(-np.random.standard_normal((B, I))))
    d = np.arange(DEG + 1)
    g = 0.5 ** d / np.sqrt(I * (DEG + 1))
    undo = np.where(d % 2 == 1, 1.0 / u[:, None, None], 1.0)
    return {"x": bf(np.log(p / (1.0 - p))),
            "alpha": bf(0.5 + 0.1 * np.random.standard_normal(1)),
            "coeffs": bf(np.random.standard_normal((I, O, DEG + 1)) * g * undo),
            "ln_weight": bf(1.0 + 0.1 * np.random.standard_normal(O)),
            "ln_bias": bf(0.1 * np.random.standard_normal(O))}


def reference(x, alpha, coeffs, ln_weight, ln_bias):
    xs = 1.0 / (1.0 + np.exp(-f64(x)))
    basis = gottlieb_basis(xs, f64(alpha), DEG)
    c = np.ascontiguousarray(f64(coeffs).transpose(2, 0, 1))
    y0 = c[0].sum(0)
    y = (mxq(basis[1:], 2, "e4m3") @ mxq(c[1:], 1, "e4m3")).sum(0) + y0
    mu = y.mean(-1, keepdims=True)
    var = np.square(y - mu).mean(-1, keepdims=True)
    y = (y - mu) / np.sqrt(var + LN_EPS)
    return y * f64(ln_weight) + f64(ln_bias)

@@ -1,0 +1,233 @@
+from contextlib import ExitStack
+
+import concourse.mybir as mybir
+from concourse.masks import make_identity
+
+F32 = mybir.dt.float32
+BF16 = mybir.dt.bfloat16
+U32 = mybir.dt.uint32
+U8 = mybir.dt.uint8
+FP8X4 = mybir.dt.float8_e4m3fn_x4
+ALU = mybir.AluOpType
+ACT = mybir.ActivationFunctionType
+
+P = 128
+B, I, O, DEG = 8192, 512, 128, 5
+NT = B // P
+G = 4
+NCH = NT // G
+CW = G * I
+NW = CW // 4
+LN_EPS = 1e-5
+FLOPS = 2 * B * I * O * DEG
+
+T1_ON_VECTOR = ()
+
+
+def tile_gottliebkanlayer_t_kernel(tc, x, alpha, coeffs, ln_weight, ln_bias, out):
+    nc = tc.nc
+    x_v = x.rearrange("(p t) i -> p (t i)", t=NT)
+    out_v = out.rearrange("(p t) o -> p (t o)", t=NT)
+    with ExitStack() as ctx:
+        const = ctx.enter_context(tc.tile_pool(name="const", bufs=1))
+        xin = ctx.enter_context(tc.tile_pool(name="xin", bufs=4))
+        work = ctx.enter_context(tc.tile_pool(name="work", bufs=2))
+        small = ctx.enter_context(tc.tile_pool(name="small", bufs=3))
+        psum = ctx.enter_context(tc.psum_pool(name="psum", bufs=2))
+
+        x_tiles = {}
+
+        def load_x(c):
+            x_sb = xin.tile([P, CW], BF16, name="x_sb")
+            nc.sync.dma_start(out=x_sb[:], in_=x_v[:, c * CW:(c + 1) * CW])
+            x_tiles[c] = x_sb
+
+        for c in range(3):
+            load_x(c)
+        a_bf = const.tile([P, 1], BF16, name="a_bf")
+        nc.scalar.dma_start(out=a_bf[:], in_=alpha.partition_broadcast(P))
+        craw = const.tile([P, 4 * O * 6], BF16, name="craw")
+        nc.scalar.dma_start(
+            out=craw[:].rearrange("p (u r) -> p u r", u=2),
+            in_=coeffs.rearrange("(u q e) o d -> q u (e o d)", u=2, e=2),
+        )
+        g_b = const.tile([P, O], BF16, name="g_b")
+        nc.scalar.dma_start(out=g_b[:], in_=ln_weight.partition_broadcast(P))
+        b_b = const.tile([P, O], BF16, name="b_b")
+        nc.scalar.dma_start(out=b_b[:], in_=ln_bias.partition_broadcast(P))
+
+        cst0 = const.tile([P, 9], F32, name="cst0")
+        nc.vector.memset(cst0[:], 2.0)
+        for k, v in ((0, 0.0), (2, 6.0), (3, 1.0), (6, 3.0), (7, 4.0), (8, 8.0)):
+            nc.vector.memset(cst0[:, k:k + 1], v)
+        cst2 = const.tile([P, 2], F32, name="cst2")
+        nc.vector.memset(cst2[:, 0:1], 2.0)
+        nc.vector.memset(cst2[:, 1:2], 8.0)
+        powe = const.tile([P, 2], F32, name="powe")
+        nc.vector.memset(powe[:, 0:1], 0.5)
+        nc.vector.memset(powe[:, 1:2], -0.5)
+        mhalf = const.tile([P, G], F32, name="mhalf")
+        nc.vector.memset(mhalf[:], -0.5)
+        ones = const.tile([P, 64], BF16, name="ones")
+        nc.vector.memset(ones[:], 1.0)
+        ident = const.tile([P, P], F32, name="ident")
+        make_identity(nc, ident[:])
+
+        sc = const.tile([P, 48], F32, name="sc")
+        names = ("a0", "a2", "a6", "a1", "a2b", "a2c", "a3", "a4", "a8", "p01", "a2sq", "c40", "c42", "c31", "c33",
+                 "c55q", "c51", "c53", "h3", "h5", "sg3", "s45", "ab3", "ab5", "r2", "r3", "rc", "v3", "t1", "u0", "u1",
+                 "w0", "w1", "m2", "e3", "x1", "b4", "nx2", "k4", "m4", "sg5", "t5", "b5", "nt", "e5", "x5", "s5", "c11")
+        idx = dict((n, k) for k, n in enumerate(names))
+        sc2 = const.tile([P, 2], F32, name="sc2")
+
+        def col(n, w=1):
+            return sc[:, idx[n]:idx[n] + w]
+
+        def ts(o, i, s1, s2=None, op0=ALU.mult, op1=ALU.mult):
+            if s2 is None:
+                nc.vector.tensor_scalar(out=o, in0=i, scalar1=s1, scalar2=None, op0=op0)
+            else:
+                nc.vector.tensor_scalar(out=o, in0=i, scalar1=s1, scalar2=s2, op0=op0, op1=op1)
+
+        ts(col("a0", 9), cst0[:], a_bf[:, 0:1], op0=ALU.add)
+        nc.vector.tensor_tensor(out=col("p01", 3), in0=col("a0", 3), in1=col("a1", 3), op=ALU.mult)
+        ts(col("c31"), col("a2sq"), -4.0, 8.0, ALU.mult, ALU.add)
+        nc.vector.scalar_tensor_tensor(out=col("c33"), in0=col("p01"), scalar=8.0, in1=col("a2"),
+                                       op0=ALU.mult, op1=ALU.mult)
+        ts(col("c55q"), col("c33"), col("a3"), col("a4"))
+        ts(col("h3", 2), col("c33", 2), 0.0, 0.5, ALU.is_ge, ALU.subtract)
+        nc.vector.tensor_tensor(out=col("sg3", 2), in0=col("h3", 2), in1=cst2[:], op=ALU.mult)
+        nc.vector.tensor_tensor(out=col("ab3", 2), in0=col("c33", 2), in1=col("sg3", 2), op=ALU.mult)
+        gp = const.tile([P, 2], F32, name="gp")
+        nc.gpsimd.tensor_tensor(out=gp[:], in0=col("ab3", 2), in1=powe[:], op=ALU.pow)
+        s3 = gp[:, 0:1]
+        ir5 = gp[:, 1:2]
+        ts(col("c11"), col("a0"), 2.0)
+        ts(sc2[:, 0:1], col("a2"), -1.0)
+        c20 = sc2[:, 0:1]
+        ts(col("v3"), col("p01"), col("a6"), -4.0)
+        ts(col("t1"), col("c31"), col("a3"), 2.0)
+        nc.vector.tensor_tensor(out=col("c42"), in0=col("t1"), in1=col("v3"), op=ALU.add)
+        nc.vector.reciprocal(out=col("r2", 2), in_=col("a2c", 2))
+        nc.vector.reciprocal(out=col("rc"), in_=col("c33"))
+        ts(col("m2"), col("r2"), col("sg3"), 0.5)
+        ts(col("e3"), col("c31"), col("sg3"))
+        ts(col("x1"), col("c42"), col("r3"), 0.25)
+        ts(col("b4"), col("x1"), col("sg3"))
+        ts(col("nx2"), col("c42"), col("rc"), -0.5)
+        nc.vector.scalar_tensor_tensor(out=col("k4"), in0=col("x1"), scalar=col("nx2"), in1=col("c40"),
+                                       op0=ALU.mult, op1=ALU.add)
+        ts(col("m4"), col("a3"), col("rc"), 2.0)
+        ts(col("u0", 2), col("c40", 2), col("a4"), 2.0)
+        ts(col("w0", 2), col("c31", 2), col("a8"))
+        nc.vector.tensor_tensor(out=col("c51", 2), in0=col("u0", 2), in1=col("w0", 2), op=ALU.subtract)
+        ts(col("sg5"), col("s45"), 0.25)
+        ts(col("t5"), col("c53"), ir5, 0.5)
+        ts(col("b5"), col("t5"), col("sg5"))
+        ts(col("nt"), col("t5"), col("t5"), -1.0)
+        nc.vector.scalar_tensor_tensor(out=col("e5"), in0=col("c51"), scalar=col("sg5"), in1=col("nt"),
+                                       op0=ALU.mult, op1=ALU.add)
+        ts(col("x5"), col("ab5"), ir5, col("rc"))
+        ts(col("s5"), col("x5"), col("sg3"))
+
+        craw4 = craw[:].rearrange("p (t o d) -> p t o d", t=4, o=O, d=6)
+        c0 = const.tile([P, 4 * O], BF16, name="c0")
+        nc.gpsimd.tensor_scalar(out=c0[:].rearrange("p (t o) -> p t o", t=4), in0=craw4[:, :, :, 0],
+                                scalar1=1.0, scalar2=1.0, op0=ALU.mult, op1=ALU.mult)
+        cg = const.tile([P, DEG * 4 * O], BF16, name="cg", align_bytes=64)
+        for d in range(1, DEG + 1):
+            sign = {3: col("sg3"), 5: col("sg5")}.get(d, 1.0)
+            nc.gpsimd.tensor_scalar(
+                out=cg[:, (d - 1) * 4 * O:d * 4 * O].rearrange("p (o t) -> p o t", t=4),
+                in0=craw4[:, :, :, d].rearrange("p t o -> p o t"),
+                scalar1=sign, scalar2=1.0, op0=ALU.mult, op1=ALU.mult)
+        ccod = const.tile([P, DEG * O], U32, name="ccod", align_bytes=64)
+        cscl = const.tile([P, DEG * O], U8, name="cscl", align_bytes=64)
+        nc.vector.quantize_mx(out=ccod[:, 0:4 * O].bitcast(FP8X4), scales=cscl[:, 0:4 * O], in_=cg[:, 0:16 * O])
+        nc.vector.quantize_mx(out=ccod[:, 4 * O:5 * O].bitcast(FP8X4), scales=cscl[:, 4 * O:5 * O],
+                              in_=cg[:, 16 * O:20 * O])
+        ps0 = psum.tile([P, 64], F32, name="ps0", tag="ycg")
+        for t in range(4):
+            nc.tensor.matmul(out=ps0[:], lhsT=c0[:, t * O:(t + 1) * O], rhs=ones[:], start=(t == 0), stop=(t == 3))
+        y0 = const.tile([P, 1], F32, name="y0")
+        nc.vector.tensor_copy(out=y0[:], in_=ps0[:, 0:1])
+        cen = const.tile([P, O], F32, name="cen")
+        ts(cen[:], ident[:], -1.0 / O, op0=ALU.add)
+        ceng = const.tile([P, O], F32, name="ceng")
+        nc.vector.tensor_tensor(out=ceng[:], in0=cen[:], in1=g_b[:], op=ALU.mult)
+
+        for c in range(NCH):
+            if c + 3 < NCH:
+                load_x(c + 3)
+            xw = x_tiles[c][:].bitcast(F32)
+            z = work.tile([P, CW], F32, name="z")
+            for h in range(G // 2):
+                xt = psum.tile([P, 512], F32, name="xt", tag="xt", bufs=3)
+                for j2 in range(2):
+                    for u in range(2):
+                        nc.tensor.transpose(
+                            xt[:, u * 256 + j2 * P:u * 256 + (j2 + 1) * P],
+                            xw[:, (2 * h + j2) * 256 + u * P:(2 * h + j2) * 256 + (u + 1) * P],
+                            ident[:])
+                nc.scalar.activation(
+                    out=z[:, h * 1024:(h + 1) * 1024].rearrange("p (n u e) -> p n u e", u=2, e=2),
+                    in_=xt[:].bitcast(BF16).rearrange("p (u n e) -> p n u e", u=2, e=2),
+                    func=ACT.Sigmoid)
+            tb = work.tile([P, DEG * CW], BF16, name="tb", align_bytes=64)
+            w3 = work.tile([P, CW], F32, name="w3")
+            nc.scalar.activation(out=w3[:], in_=z[:], func=ACT.Square, scale=s3)
+            if c in T1_ON_VECTOR:
+                ts(tb[:, 0:CW], z[:], col("c11"))
+            else:
+                nc.scalar.activation(out=tb[:, 0:CW], in_=z[:], func=ACT.Copy, scale=col("c11"))
+            p4 = work.tile([P, CW], F32, name="p4")
+            nc.scalar.activation(out=p4[:], in_=w3[:], func=ACT.Square, bias=col("b4"))
+            p5 = work.tile([P, CW], F32, name="p5")
+            nc.scalar.activation(out=p5[:], in_=w3[:], func=ACT.Square, scale=col("s5"), bias=col("b5"))
+            ts(tb[:, CW:2 * CW], w3[:], col("m2"), c20, ALU.mult, ALU.add)
+            nc.vector.scalar_tensor_tensor(out=tb[:, 2 * CW:3 * CW], in0=w3[:], scalar=col("e3"), in1=z[:],
+                                           op0=ALU.add, op1=ALU.mult)
+            cod = work.tile([P, DEG * NW], U32, name="cod", align_bytes=64)
+            scl = work.tile([P, DEG * NW], U8, name="scl", align_bytes=64)
+
+            def quant(d0, d1):
+                nc.vector.quantize_mx(out=cod[:, d0 * NW:d1 * NW].bitcast(FP8X4), scales=scl[:, d0 * NW:d1 * NW],
+                                      in_=tb[:, d0 * CW:d1 * CW])
+
+            quant(0, 2)
+            ts(tb[:, 3 * CW:4 * CW], p4[:], col("m4"), col("k4"), ALU.mult, ALU.add)
+            nc.vector.scalar_tensor_tensor(out=tb[:, 4 * CW:5 * CW], in0=p5[:], scalar=col("e5"), in1=z[:],
+                                           op0=ALU.add, op1=ALU.mult)
+            quant(2, 4)
+            quant(4, 5)
+
+            yt = psum.tile([P, NW], F32, name="yt", tag="yt", bufs=2)
+            for d in range(DEG):
+                nc.tensor.matmul_mx(
+                    out=yt[:],
+                    lhsT=ccod[:, d * O:(d + 1) * O].bitcast(FP8X4), lhsT_scale=cscl[:, d * O:(d + 1) * O],
+                    rhs=cod[:, d * NW:(d + 1) * NW].bitcast(FP8X4), rhs_scale=scl[:, d * NW:(d + 1) * NW],
+                    start=(d == 0), stop=(d == DEG - 1))
+            yts = small.tile([P, NW], F32, name="yts")
+            nc.scalar.activation(out=yts[:], in_=yt[:], func=ACT.Identity, bias=y0[:, 0:1])
+            yst = psum.tile([P, NW], F32, name="yst", tag="yst", bufs=1)
+            for j in range(G):
+                nc.tensor.transpose(yst[:, j * O:(j + 1) * O], yts[:, j * P:(j + 1) * P], ident[:])
+            st = small.tile([P, G, 6], F32, name="st")
+            mv = small.tile([P, G, 2], F32, name="mv")
+            for j in range(G):
+                nc.vector.bn_stats(out=st[:, j, :], in_=yst[:, j * O:(j + 1) * O])
+                nc.vector.bn_aggr(out=mv[:, j, :], in_=st[:, j, :])
+            ve = small.tile([P, G], F32, name="ve")
+            ts(ve[:], mv[:, :, 1], LN_EPS, op0=ALU.add)
+            rstd = small.tile([P, G], F32, name="rstd")
+            nc.gpsimd.tensor_tensor(out=rstd[:], in0=ve[:], in1=mhalf[:], op=ALU.pow)
+            ycg = psum.tile([P, NW], F32, name="ycg", tag="ycg", bufs=2)
+            for j in range(G):
+                nc.tensor.matmul(out=ycg[:, j * O:(j + 1) * O], lhsT=yts[:, j * P:(j + 1) * P], rhs=ceng[:],
+                                 start=True, stop=True)
+            osb = small.tile([P, G * O], F32, name="osb")
+            for j in range(G):
+                nc.vector.scalar_tensor_tensor(out=osb[:, j * O:(j + 1) * O], in0=ycg[:, j * O:(j + 1) * O],
+                                               scalar=rstd[:, j:j + 1], in1=b_b[:], op0=ALU.mult, op1=ALU.add)
+            nc.sync.dma_start(out=out_v[:, c * G * O:(c + 1) * G * O], in_=osb[:])

@@ -21,7 +21,7 @@ NW = CW // 4
 LN_EPS = 1e-5
 FLOPS = 2 * B * I * O * DEG
 
-T1_ON_VECTOR = ()
+T1_ON_VECTOR = (3, 7, 11, 15)
 
 
 def tile_gottliebkanlayer_t_kernel(tc, x, alpha, coeffs, ln_weight, ln_bias, out):
@@ -34,6 +34,7 @@ def tile_gottliebkanlayer_t_kernel(tc, x, alpha, coeffs, ln_weight, ln_bias, out
         work = ctx.enter_context(tc.tile_pool(name="work", bufs=2))
         small = ctx.enter_context(tc.tile_pool(name="small", bufs=3))
         psum = ctx.enter_context(tc.psum_pool(name="psum", bufs=2))
+        ctx.enter_context(tc.manual_schedule())
 
         x_tiles = {}
 
@@ -42,7 +43,7 @@ def tile_gottliebkanlayer_t_kernel(tc, x, alpha, coeffs, ln_weight, ln_bias, out
             nc.sync.dma_start(out=x_sb[:], in_=x_v[:, c * CW:(c + 1) * CW])
             x_tiles[c] = x_sb
 
-        for c in range(3):
+        for c in range(4):
             load_x(c)
         a_bf = const.tile([P, 1], BF16, name="a_bf")
         nc.scalar.dma_start(out=a_bf[:], in_=alpha.partition_broadcast(P))
@@ -130,6 +131,124 @@ def tile_gottliebkanlayer_t_kernel(tc, x, alpha, coeffs, ln_weight, ln_bias, out
         ts(col("x5"), col("ab5"), ir5, col("rc"))
         ts(col("s5"), col("x5"), col("sg3"))
 
+
+        xts = {}
+        zs = {}
+        w3s = {}
+        p4s = {}
+        p5s = {}
+        tbs = {}
+        cods = {}
+        scls = {}
+        yt_ps = {}
+        ytss = {}
+        ysts = {}
+        rstds = {}
+        ycgs = {}
+
+        def x_transposes(c):
+            xw = x_tiles[c][:].bitcast(F32)
+            for h in range(G // 2):
+                xt = psum.tile([P, 512], F32, name="xt", tag="xt")
+                for j2 in range(2):
+                    for u in range(2):
+                        nc.tensor.transpose(
+                            xt[:, u * 256 + j2 * P:u * 256 + (j2 + 1) * P],
+                            xw[:, (2 * h + j2) * 256 + u * P:(2 * h + j2) * 256 + (u + 1) * P],
+                            ident[:])
+                xts[(c, h)] = xt
+
+        def sigmoid(c):
+            z = work.tile([P, CW], F32, name="z")
+            for h in range(G // 2):
+                nc.scalar.activation(
+                    out=z[:, h * 1024:(h + 1) * 1024].rearrange("p (n u e) -> p n u e", u=2, e=2),
+                    in_=xts[(c, h)][:].bitcast(BF16).rearrange("p (u n e) -> p n u e", u=2, e=2),
+                    func=ACT.Sigmoid)
+            zs[c] = z
+
+        def squares(c):
+            w3 = work.tile([P, CW], F32, name="w3")
+            nc.scalar.activation(out=w3[:], in_=zs[c][:], func=ACT.Square, scale=s3)
+            p4 = work.tile([P, CW], F32, name="p4")
+            nc.scalar.activation(out=p4[:], in_=w3[:], func=ACT.Square, bias=col("b4"))
+            p5 = work.tile([P, CW], F32, name="p5")
+            nc.scalar.activation(out=p5[:], in_=w3[:], func=ACT.Square, scale=col("s5"), bias=col("b5"))
+            w3s[c], p4s[c], p5s[c] = w3, p4, p5
+            tbs[c] = work.tile([P, DEG * CW], BF16, name="tb", align_bytes=64)
+
+        def t1_scalar(c):
+            if c not in T1_ON_VECTOR:
+                nc.scalar.activation(out=tbs[c][:, 0:CW], in_=zs[c][:], func=ACT.Copy, scale=col("c11"))
+
+        def basis(c):
+            tb, z, w3 = tbs[c], zs[c], w3s[c]
+            ts(tb[:, CW:2 * CW], w3[:], col("m2"), c20, ALU.mult, ALU.add)
+            nc.vector.scalar_tensor_tensor(out=tb[:, 2 * CW:3 * CW], in0=w3[:], scalar=col("e3"), in1=z[:],
+                                           op0=ALU.add, op1=ALU.mult)
+            ts(tb[:, 3 * CW:4 * CW], p4s[c][:], col("m4"), col("k4"), ALU.mult, ALU.add)
+            nc.vector.scalar_tensor_tensor(out=tb[:, 4 * CW:5 * CW], in0=p5s[c][:], scalar=col("e5"), in1=z[:],
+                                           op0=ALU.add, op1=ALU.mult)
+            if c in T1_ON_VECTOR:
+                ts(tb[:, 0:CW], z[:], col("c11"))
+
+        def quantise(c):
+            cod = work.tile([P, DEG * NW], U32, name="cod", align_bytes=64)
+            scl = work.tile([P, DEG * NW], U8, name="scl", align_bytes=64)
+            for d0, d1 in ((2, 4), (4, 5), (0, 2)):
+                nc.vector.quantize_mx(out=cod[:, d0 * NW:d1 * NW].bitcast(FP8X4), scales=scl[:, d0 * NW:d1 * NW],
+                                      in_=tbs[c][:, d0 * CW:d1 * CW])
+            cods[c], scls[c] = cod, scl
+
+        def mx(c):
+            yt = psum.tile([P, NW], F32, name="yt", tag="yt")
+            order = (2, 3, 4, 0, 1)
+            for n, d in enumerate(order):
+                nc.tensor.matmul_mx(
+                    out=yt[:],
+                    lhsT=ccod[:, d * O:(d + 1) * O].bitcast(FP8X4), lhsT_scale=cscl[:, d * O:(d + 1) * O],
+                    rhs=cods[c][:, d * NW:(d + 1) * NW].bitcast(FP8X4), rhs_scale=scls[c][:, d * NW:(d + 1) * NW],
+                    start=(n == 0), stop=(n == DEG - 1))
+            yt_ps[c] = yt
+
+        def evacuate(c):
+            yts = small.tile([P, NW], F32, name="yts")
+            nc.scalar.activation(out=yts[:], in_=yt_ps[c][:], func=ACT.Identity, bias=y0[:, 0:1])
+            ytss[c] = yts
+
+        def y_transposes(c):
+            yst = psum.tile([P, NW], F32, name="yst", tag="yst")
+            for j in range(G):
+                nc.tensor.transpose(yst[:, j * O:(j + 1) * O], ytss[c][:, j * P:(j + 1) * P], ident[:])
+            ysts[c] = yst
+
+        def stats(c):
+            st = small.tile([P, G, 6], F32, name="st")
+            mv = small.tile([P, G, 2], F32, name="mv")
+            for j in range(G):
+                nc.vector.bn_stats(out=st[:, j, :], in_=ysts[c][:, j * O:(j + 1) * O])
+            for j in range(G):
+                nc.vector.bn_aggr(out=mv[:, j, :], in_=st[:, j, :])
+            ve = small.tile([P, G], F32, name="ve")
+            ts(ve[:], mv[:, :, 1], LN_EPS, op0=ALU.add)
+            rstd = small.tile([P, G], F32, name="rstd")
+            nc.gpsimd.tensor_tensor(out=rstd[:], in0=ve[:], in1=mhalf[:], op=ALU.pow)
+            rstds[c] = rstd
+
+        def centre(c):
+            ycg = psum.tile([P, NW], F32, name="ycg", tag="ycg")
+            for j in range(G):
+                nc.tensor.matmul(out=ycg[:, j * O:(j + 1) * O], lhsT=ytss[c][:, j * P:(j + 1) * P], rhs=ceng[:],
+                                 start=True, stop=True)
+            ycgs[c] = ycg
+
+        def final(c):
+            osb = small.tile([P, G * O], F32, name="osb")
+            for j in range(G):
+                nc.vector.scalar_tensor_tensor(out=osb[:, j * O:(j + 1) * O], in0=ycgs[c][:, j * O:(j + 1) * O],
+                                               scalar=rstds[c][:, j:j + 1], in1=b_b[:], op0=ALU.mult, op1=ALU.add)
+            nc.sync.dma_start(out=out_v[:, c * G * O:(c + 1) * G * O], in_=osb[:])
+
         craw4 = craw[:].rearrange("p (t o d) -> p t o d", t=4, o=O, d=6)
         c0 = const.tile([P, 4 * O], BF16, name="c0")
         nc.gpsimd.tensor_scalar(out=c0[:].rearrange("p (t o) -> p t o", t=4), in0=craw4[:, :, :, 0],
@@ -143,91 +262,47 @@ def tile_gottliebkanlayer_t_kernel(tc, x, alpha, coeffs, ln_weight, ln_bias, out
                 scalar1=sign, scalar2=1.0, op0=ALU.mult, op1=ALU.mult)
         ccod = const.tile([P, DEG * O], U32, name="ccod", align_bytes=64)
         cscl = const.tile([P, DEG * O], U8, name="cscl", align_bytes=64)
-        nc.vector.quantize_mx(out=ccod[:, 0:4 * O].bitcast(FP8X4), scales=cscl[:, 0:4 * O], in_=cg[:, 0:16 * O])
-        nc.vector.quantize_mx(out=ccod[:, 4 * O:5 * O].bitcast(FP8X4), scales=cscl[:, 4 * O:5 * O],
-                              in_=cg[:, 16 * O:20 * O])
-        ps0 = psum.tile([P, 64], F32, name="ps0", tag="ycg")
-        for t in range(4):
-            nc.tensor.matmul(out=ps0[:], lhsT=c0[:, t * O:(t + 1) * O], rhs=ones[:], start=(t == 0), stop=(t == 3))
         y0 = const.tile([P, 1], F32, name="y0")
-        nc.vector.tensor_copy(out=y0[:], in_=ps0[:, 0:1])
         cen = const.tile([P, O], F32, name="cen")
-        ts(cen[:], ident[:], -1.0 / O, op0=ALU.add)
         ceng = const.tile([P, O], F32, name="ceng")
-        nc.vector.tensor_tensor(out=ceng[:], in0=cen[:], in1=g_b[:], op=ALU.mult)
 
-        for c in range(NCH):
-            if c + 3 < NCH:
-                load_x(c + 3)
-            xw = x_tiles[c][:].bitcast(F32)
-            z = work.tile([P, CW], F32, name="z")
-            for h in range(G // 2):
-                xt = psum.tile([P, 512], F32, name="xt", tag="xt", bufs=3)
-                for j2 in range(2):
-                    for u in range(2):
-                        nc.tensor.transpose(
-                            xt[:, u * 256 + j2 * P:u * 256 + (j2 + 1) * P],
-                            xw[:, (2 * h + j2) * 256 + u * P:(2 * h + j2) * 256 + (u + 1) * P],
-                            ident[:])
-                nc.scalar.activation(
-                    out=z[:, h * 1024:(h + 1) * 1024].rearrange("p (n u e) -> p n u e", u=2, e=2),
-                    in_=xt[:].bitcast(BF16).rearrange("p (u n e) -> p n u e", u=2, e=2),
-                    func=ACT.Sigmoid)
-            tb = work.tile([P, DEG * CW], BF16, name="tb", align_bytes=64)
-            w3 = work.tile([P, CW], F32, name="w3")
-            nc.scalar.activation(out=w3[:], in_=z[:], func=ACT.Square, scale=s3)
-            if c in T1_ON_VECTOR:
-                ts(tb[:, 0:CW], z[:], col("c11"))
-            else:
-                nc.scalar.activation(out=tb[:, 0:CW], in_=z[:], func=ACT.Copy, scale=col("c11"))
-            p4 = work.tile([P, CW], F32, name="p4")
-            nc.scalar.activation(out=p4[:], in_=w3[:], func=ACT.Square, bias=col("b4"))
-            p5 = work.tile([P, CW], F32, name="p5")
-            nc.scalar.activation(out=p5[:], in_=w3[:], func=ACT.Square, scale=col("s5"), bias=col("b5"))
-            ts(tb[:, CW:2 * CW], w3[:], col("m2"), c20, ALU.mult, ALU.add)
-            nc.vector.scalar_tensor_tensor(out=tb[:, 2 * CW:3 * CW], in0=w3[:], scalar=col("e3"), in1=z[:],
-                                           op0=ALU.add, op1=ALU.mult)
-            cod = work.tile([P, DEG * NW], U32, name="cod", align_bytes=64)
-            scl = work.tile([P, DEG * NW], U8, name="scl", align_bytes=64)
+        def coefficient_work():
+            nc.vector.quantize_mx(out=ccod[:, 0:4 * O].bitcast(FP8X4), scales=cscl[:, 0:4 * O], in_=cg[:, 0:16 * O])
+            nc.vector.quantize_mx(out=ccod[:, 4 * O:5 * O].bitcast(FP8X4), scales=cscl[:, 4 * O:5 * O],
+                                  in_=cg[:, 16 * O:20 * O])
+            ps0 = psum.tile([P, 64], F32, name="ps0", tag="ycg")
+            for t in range(4):
+                nc.tensor.matmul(out=ps0[:], lhsT=c0[:, t * O:(t + 1) * O], rhs=ones[:], start=(t == 0),
+                                 stop=(t == 3))
+            nc.vector.tensor_copy(out=y0[:], in_=ps0[:, 0:1])
+            ts(cen[:], ident[:], -1.0 / O, op0=ALU.add)
+            nc.vector.tensor_tensor(out=ceng[:], in0=cen[:], in1=g_b[:], op=ALU.mult)
 
-            def quant(d0, d1):
-                nc.vector.quantize_mx(out=cod[:, d0 * NW:d1 * NW].bitcast(FP8X4), scales=scl[:, d0 * NW:d1 * NW],
-                                      in_=tb[:, d0 * CW:d1 * CW])
-
-            quant(0, 2)
-            ts(tb[:, 3 * CW:4 * CW], p4[:], col("m4"), col("k4"), ALU.mult, ALU.add)
-            nc.vector.scalar_tensor_tensor(out=tb[:, 4 * CW:5 * CW], in0=p5[:], scalar=col("e5"), in1=z[:],
-                                           op0=ALU.add, op1=ALU.mult)
-            quant(2, 4)
-            quant(4, 5)
-
-            yt = psum.tile([P, NW], F32, name="yt", tag="yt", bufs=2)
-            for d in range(DEG):
-                nc.tensor.matmul_mx(
-                    out=yt[:],
-                    lhsT=ccod[:, d * O:(d + 1) * O].bitcast(FP8X4), lhsT_scale=cscl[:, d * O:(d + 1) * O],
-                    rhs=cod[:, d * NW:(d + 1) * NW].bitcast(FP8X4), rhs_scale=scl[:, d * NW:(d + 1) * NW],
-                    start=(d == 0), stop=(d == DEG - 1))
-            yts = small.tile([P, NW], F32, name="yts")
-            nc.scalar.activation(out=yts[:], in_=yt[:], func=ACT.Identity, bias=y0[:, 0:1])
-            yst = psum.tile([P, NW], F32, name="yst", tag="yst", bufs=1)
-            for j in range(G):
-                nc.tensor.transpose(yst[:, j * O:(j + 1) * O], yts[:, j * P:(j + 1) * P], ident[:])
-            st = small.tile([P, G, 6], F32, name="st")
-            mv = small.tile([P, G, 2], F32, name="mv")
-            for j in range(G):
-                nc.vector.bn_stats(out=st[:, j, :], in_=yst[:, j * O:(j + 1) * O])
-                nc.vector.bn_aggr(out=mv[:, j, :], in_=st[:, j, :])
-            ve = small.tile([P, G], F32, name="ve")
-            ts(ve[:], mv[:, :, 1], LN_EPS, op0=ALU.add)
-            rstd = small.tile([P, G], F32, name="rstd")
-            nc.gpsimd.tensor_tensor(out=rstd[:], in0=ve[:], in1=mhalf[:], op=ALU.pow)
-            ycg = psum.tile([P, NW], F32, name="ycg", tag="ycg", bufs=2)
-            for j in range(G):
-                nc.tensor.matmul(out=ycg[:, j * O:(j + 1) * O], lhsT=yts[:, j * P:(j + 1) * P], rhs=ceng[:],
-                                 start=True, stop=True)
-            osb = small.tile([P, G * O], F32, name="osb")
-            for j in range(G):
-                nc.vector.scalar_tensor_tensor(out=osb[:, j * O:(j + 1) * O], in0=ycg[:, j * O:(j + 1) * O],
-                                               scalar=rstd[:, j:j + 1], in1=b_b[:], op0=ALU.mult, op1=ALU.add)
-            nc.sync.dma_start(out=out_v[:, c * G * O:(c + 1) * G * O], in_=osb[:])
+        x_transposes(0)
+        for k in range(NCH + 2):
+            if k < NCH:
+                sigmoid(k)
+                if k + 1 < NCH:
+                    x_transposes(k + 1)
+                if k + 4 < NCH:
+                    load_x(k + 4)
+            if 0 <= k - 2:
+                centre(k - 2)
+            if 0 <= k - 1 < NCH:
+                mx(k - 1)
+            if k < NCH:
+                squares(k)
+            if 0 <= k - 1 < NCH:
+                evacuate(k - 1)
+                y_transposes(k - 1)
+            if k < NCH:
+                t1_scalar(k)
+                basis(k)
+            if k == 0:
+                coefficient_work()
+            if 0 <= k - 1 < NCH:
+                stats(k - 1)
+            if 0 <= k - 2:
+                final(k - 2)
+            if k < NCH:
+                quantise(k)

@@ -15,13 +15,16 @@ P = 128
 B, I, O, DEG = 8192, 512, 128, 5
 NT = B // P
 G = 4
-NCH = NT // G
+SIZES = (2, 2) + (4,) * 14 + (2, 1, 1)
+NCH = len(SIZES)
+STARTS = tuple(sum(SIZES[:c]) for c in range(NCH))
+assert sum(SIZES) == NT
 CW = G * I
 NW = CW // 4
 LN_EPS = 1e-5
 FLOPS = 2 * B * I * O * DEG
 
-T1_ON_VECTOR = (3, 7, 11, 15)
+T1_VECTOR_COLS = tuple(g * I if c < 2 else (0 if c >= NCH - 3 else 256 * g // G) for c, g in enumerate(SIZES))
 
 
 def tile_gottliebkanlayer_t_kernel(tc, x, alpha, coeffs, ln_weight, ln_bias, out):
@@ -33,6 +36,7 @@ def tile_gottliebkanlayer_t_kernel(tc, x, alpha, coeffs, ln_weight, ln_bias, out
         xin = ctx.enter_context(tc.tile_pool(name="xin", bufs=4))
         work = ctx.enter_context(tc.tile_pool(name="work", bufs=2))
         small = ctx.enter_context(tc.tile_pool(name="small", bufs=3))
+        stat = ctx.enter_context(tc.tile_pool(name="stat", bufs=5))
         psum = ctx.enter_context(tc.psum_pool(name="psum", bufs=2))
         ctx.enter_context(tc.manual_schedule())
 
@@ -40,7 +44,7 @@ def tile_gottliebkanlayer_t_kernel(tc, x, alpha, coeffs, ln_weight, ln_bias, out
 
         def load_x(c):
             x_sb = xin.tile([P, CW], BF16, name="x_sb")
-            nc.sync.dma_start(out=x_sb[:], in_=x_v[:, c * CW:(c + 1) * CW])
+            nc.sync.dma_start(out=x_sb[:, 0:SIZES[c] * I], in_=x_v[:, STARTS[c] * I:(STARTS[c] + SIZES[c]) * I])
             x_tiles[c] = x_sb
 
         for c in range(4):
@@ -61,12 +65,11 @@ def tile_gottliebkanlayer_t_kernel(tc, x, alpha, coeffs, ln_weight, ln_bias, out
         nc.vector.memset(cst0[:], 2.0)
         for k, v in ((0, 0.0), (2, 6.0), (3, 1.0), (6, 3.0), (7, 4.0), (8, 8.0)):
             nc.vector.memset(cst0[:, k:k + 1], v)
-        cst2 = const.tile([P, 2], F32, name="cst2")
-        nc.vector.memset(cst2[:, 0:1], 2.0)
-        nc.vector.memset(cst2[:, 1:2], 8.0)
-        powe = const.tile([P, 2], F32, name="powe")
-        nc.vector.memset(powe[:, 0:1], 0.5)
-        nc.vector.memset(powe[:, 1:2], -0.5)
+        floors = const.tile([P, 3], F32, name="floors")
+        powe = const.tile([P, 3], F32, name="powe")
+        for k, (lo, ex) in enumerate(((1e-4, 0.5), (6e-3, 1.0), (5e-2, -0.5))):
+            nc.vector.memset(floors[:, k:k + 1], lo)
+            nc.vector.memset(powe[:, k:k + 1], ex)
         mhalf = const.tile([P, G], F32, name="mhalf")
         nc.vector.memset(mhalf[:], -0.5)
         ones = const.tile([P, 64], BF16, name="ones")
@@ -74,12 +77,12 @@ def tile_gottliebkanlayer_t_kernel(tc, x, alpha, coeffs, ln_weight, ln_bias, out
         ident = const.tile([P, P], F32, name="ident")
         make_identity(nc, ident[:])
 
-        sc = const.tile([P, 48], F32, name="sc")
         names = ("a0", "a2", "a6", "a1", "a2b", "a2c", "a3", "a4", "a8", "p01", "a2sq", "c40", "c42", "c31", "c33",
-                 "c55q", "c51", "c53", "h3", "h5", "sg3", "s45", "ab3", "ab5", "r2", "r3", "rc", "v3", "t1", "u0", "u1",
-                 "w0", "w1", "m2", "e3", "x1", "b4", "nx2", "k4", "m4", "sg5", "t5", "b5", "nt", "e5", "x5", "s5", "c11")
+                 "c44", "c55", "c51", "c53", "h3", "h4", "h5", "sg3", "sg4", "sg5", "aa3", "aa4", "aa5", "ab3", "ab4",
+                 "ab5", "r3", "r4", "r5", "v3", "t1", "u0", "u1", "w0", "w1", "m2", "e3", "x1", "b4", "yy", "k4", "mm",
+                 "m4", "t5", "b5", "nt", "e5", "s5", "c11", "c20")
+        sc = const.tile([P, len(names)], F32, name="sc")
         idx = dict((n, k) for k, n in enumerate(names))
-        sc2 = const.tile([P, 2], F32, name="sc2")
 
         def col(n, w=1):
             return sc[:, idx[n]:idx[n] + w]
@@ -90,47 +93,46 @@ def tile_gottliebkanlayer_t_kernel(tc, x, alpha, coeffs, ln_weight, ln_bias, out
             else:
                 nc.vector.tensor_scalar(out=o, in0=i, scalar1=s1, scalar2=s2, op0=op0, op1=op1)
 
+        def stt(o, i0, s, i1, op0, op1):
+            nc.vector.scalar_tensor_tensor(out=o, in0=i0, scalar=s, in1=i1, op0=op0, op1=op1)
+
         ts(col("a0", 9), cst0[:], a_bf[:, 0:1], op0=ALU.add)
         nc.vector.tensor_tensor(out=col("p01", 3), in0=col("a0", 3), in1=col("a1", 3), op=ALU.mult)
-        ts(col("c31"), col("a2sq"), -4.0, 8.0, ALU.mult, ALU.add)
-        nc.vector.scalar_tensor_tensor(out=col("c33"), in0=col("p01"), scalar=8.0, in1=col("a2"),
-                                       op0=ALU.mult, op1=ALU.mult)
-        ts(col("c55q"), col("c33"), col("a3"), col("a4"))
-        ts(col("h3", 2), col("c33", 2), 0.0, 0.5, ALU.is_ge, ALU.subtract)
-        nc.vector.tensor_tensor(out=col("sg3", 2), in0=col("h3", 2), in1=cst2[:], op=ALU.mult)
-        nc.vector.tensor_tensor(out=col("ab3", 2), in0=col("c33", 2), in1=col("sg3", 2), op=ALU.mult)
-        gp = const.tile([P, 2], F32, name="gp")
-        nc.gpsimd.tensor_tensor(out=gp[:], in0=col("ab3", 2), in1=powe[:], op=ALU.pow)
+        stt(col("c33"), col("p01"), 8.0, col("a2"), ALU.mult, ALU.mult)
+        ts(col("c44"), col("c33"), col("a3"), 2.0)
+        ts(col("c55"), col("c44"), col("a4"), 2.0)
+        ts(col("h3", 3), col("c33", 3), 0.0, 0.5, ALU.is_ge, ALU.subtract)
+        stt(col("aa3", 3), col("c33", 3), 2.0, col("h3", 3), ALU.mult, ALU.mult)
+        nc.vector.tensor_tensor(out=col("ab3", 3), in0=col("aa3", 3), in1=floors[:], op=ALU.max)
+        gp = const.tile([P, 3], F32, name="gp")
+        nc.gpsimd.tensor_tensor(out=gp[:], in0=col("ab3", 3), in1=powe[:], op=ALU.pow)
         s3 = gp[:, 0:1]
-        ir5 = gp[:, 1:2]
+        ir5 = gp[:, 2:3]
         ts(col("c11"), col("a0"), 2.0)
-        ts(sc2[:, 0:1], col("a2"), -1.0)
-        c20 = sc2[:, 0:1]
+        ts(col("c20"), col("a2"), -1.0)
+        c20 = col("c20")
+        ts(col("sg3", 3), col("h3", 3), 2.0)
+        nc.vector.reciprocal(out=col("r3", 3), in_=col("ab3", 3))
+        ts(col("c31"), col("a2sq"), -4.0, 8.0, ALU.mult, ALU.add)
         ts(col("v3"), col("p01"), col("a6"), -4.0)
         ts(col("t1"), col("c31"), col("a3"), 2.0)
         nc.vector.tensor_tensor(out=col("c42"), in0=col("t1"), in1=col("v3"), op=ALU.add)
-        nc.vector.reciprocal(out=col("r2", 2), in_=col("a2c", 2))
-        nc.vector.reciprocal(out=col("rc"), in_=col("c33"))
-        ts(col("m2"), col("r2"), col("sg3"), 0.5)
+        ts(col("m2"), col("p01"), col("r3"), 4.0)
         ts(col("e3"), col("c31"), col("sg3"))
-        ts(col("x1"), col("c42"), col("r3"), 0.25)
-        ts(col("b4"), col("x1"), col("sg3"))
-        ts(col("nx2"), col("c42"), col("rc"), -0.5)
-        nc.vector.scalar_tensor_tensor(out=col("k4"), in0=col("x1"), scalar=col("nx2"), in1=col("c40"),
-                                       op0=ALU.mult, op1=ALU.add)
-        ts(col("m4"), col("a3"), col("rc"), 2.0)
+        ts(col("x1"), col("c42"), col("r4"), 0.5)
+        ts(col("b4"), col("x1"), col("ab3"), col("sg4"))
         ts(col("u0", 2), col("c40", 2), col("a4"), 2.0)
         ts(col("w0", 2), col("c31", 2), col("a8"))
         nc.vector.tensor_tensor(out=col("c51", 2), in0=col("u0", 2), in1=col("w0", 2), op=ALU.subtract)
-        ts(col("sg5"), col("s45"), 0.25)
         ts(col("t5"), col("c53"), ir5, 0.5)
+        ts(col("s5"), col("ab5"), ir5, col("r3"))
         ts(col("b5"), col("t5"), col("sg5"))
+        ts(col("yy"), col("x1"), col("c42"), col("sg4"))
+        stt(col("k4"), col("yy"), -0.5, col("c40"), ALU.mult, ALU.add)
+        ts(col("mm"), col("r3"), col("r3"), col("ab4"))
+        ts(col("m4"), col("mm"), col("sg4"))
         ts(col("nt"), col("t5"), col("t5"), -1.0)
-        nc.vector.scalar_tensor_tensor(out=col("e5"), in0=col("c51"), scalar=col("sg5"), in1=col("nt"),
-                                       op0=ALU.mult, op1=ALU.add)
-        ts(col("x5"), col("ab5"), ir5, col("rc"))
-        ts(col("s5"), col("x5"), col("sg3"))
-
+        stt(col("e5"), col("c51"), col("sg5"), col("nt"), ALU.mult, ALU.add)
 
         xts = {}
         zs = {}
@@ -145,109 +147,134 @@ def tile_gottliebkanlayer_t_kernel(tc, x, alpha, coeffs, ln_weight, ln_bias, out
         ysts = {}
         rstds = {}
         ycgs = {}
+        mvs = {}
+        osbs = {}
 
         def x_transposes(c):
             xw = x_tiles[c][:].bitcast(F32)
-            for h in range(G // 2):
+            for h in range((SIZES[c] + 1) // 2):
+                m = min(2, SIZES[c] - 2 * h)
                 xt = psum.tile([P, 512], F32, name="xt", tag="xt")
-                for j2 in range(2):
+                for j2 in range(m):
                     for u in range(2):
                         nc.tensor.transpose(
-                            xt[:, u * 256 + j2 * P:u * 256 + (j2 + 1) * P],
+                            xt[:, (u * m + j2) * P:(u * m + j2 + 1) * P],
                             xw[:, (2 * h + j2) * 256 + u * P:(2 * h + j2) * 256 + (u + 1) * P],
                             ident[:])
                 xts[(c, h)] = xt
 
         def sigmoid(c):
             z = work.tile([P, CW], F32, name="z")
-            for h in range(G // 2):
+            for h in range((SIZES[c] + 1) // 2):
+                m = min(2, SIZES[c] - 2 * h)
                 nc.scalar.activation(
-                    out=z[:, h * 1024:(h + 1) * 1024].rearrange("p (n u e) -> p n u e", u=2, e=2),
-                    in_=xts[(c, h)][:].bitcast(BF16).rearrange("p (u n e) -> p n u e", u=2, e=2),
+                    out=z[:, h * 1024:h * 1024 + m * I].rearrange("p (n u e) -> p n u e", u=2, e=2),
+                    in_=xts[(c, h)][:].bitcast(BF16)[:, 0:4 * m * P].rearrange("p (u n e) -> p n u e", u=2, e=2),
                     func=ACT.Sigmoid)
             zs[c] = z
 
-        def squares(c):
+        def square_w3(c):
             w3 = work.tile([P, CW], F32, name="w3")
-            nc.scalar.activation(out=w3[:], in_=zs[c][:], func=ACT.Square, scale=s3)
+            cw = SIZES[c] * I
+            nc.scalar.activation(out=w3[:, 0:cw], in_=zs[c][:, 0:cw], func=ACT.Square, scale=s3)
+            w3s[c] = w3
+
+        def squares_p4_p5(c):
+            w3 = w3s[c]
+            cw = SIZES[c] * I
             p4 = work.tile([P, CW], F32, name="p4")
-            nc.scalar.activation(out=p4[:], in_=w3[:], func=ACT.Square, bias=col("b4"))
+            nc.scalar.activation(out=p4[:, 0:cw], in_=w3[:, 0:cw], func=ACT.Square, bias=col("b4"))
             p5 = work.tile([P, CW], F32, name="p5")
-            nc.scalar.activation(out=p5[:], in_=w3[:], func=ACT.Square, scale=col("s5"), bias=col("b5"))
-            w3s[c], p4s[c], p5s[c] = w3, p4, p5
+            nc.scalar.activation(out=p5[:, 0:cw], in_=w3[:, 0:cw], func=ACT.Square, scale=col("s5"), bias=col("b5"))
+            p4s[c], p5s[c] = p4, p5
             tbs[c] = work.tile([P, DEG * CW], BF16, name="tb", align_bytes=64)
 
         def t1_scalar(c):
-            if c not in T1_ON_VECTOR:
-                nc.scalar.activation(out=tbs[c][:, 0:CW], in_=zs[c][:], func=ACT.Copy, scale=col("c11"))
+            cw, fc = SIZES[c] * I, T1_VECTOR_COLS[c]
+            if fc < cw:
+                nc.scalar.activation(out=tbs[c][:, fc:cw], in_=zs[c][:, fc:cw], func=ACT.Copy, scale=col("c11"))
 
         def basis(c):
             tb, z, w3 = tbs[c], zs[c], w3s[c]
-            ts(tb[:, CW:2 * CW], w3[:], col("m2"), c20, ALU.mult, ALU.add)
-            nc.vector.scalar_tensor_tensor(out=tb[:, 2 * CW:3 * CW], in0=w3[:], scalar=col("e3"), in1=z[:],
+            cw, fc = SIZES[c] * I, T1_VECTOR_COLS[c]
+            ts(tb[:, cw:2 * cw], w3[:, 0:cw], col("m2"), c20, ALU.mult, ALU.add)
+            nc.vector.scalar_tensor_tensor(out=tb[:, 2 * cw:3 * cw], in0=w3[:, 0:cw], scalar=col("e3"), in1=z[:, 0:cw],
                                            op0=ALU.add, op1=ALU.mult)
-            ts(tb[:, 3 * CW:4 * CW], p4s[c][:], col("m4"), col("k4"), ALU.mult, ALU.add)
-            nc.vector.scalar_tensor_tensor(out=tb[:, 4 * CW:5 * CW], in0=p5s[c][:], scalar=col("e5"), in1=z[:],
-                                           op0=ALU.add, op1=ALU.mult)
-            if c in T1_ON_VECTOR:
-                ts(tb[:, 0:CW], z[:], col("c11"))
+            ts(tb[:, 3 * cw:4 * cw], p4s[c][:, 0:cw], col("m4"), col("k4"), ALU.mult, ALU.add)
+            nc.vector.scalar_tensor_tensor(out=tb[:, 4 * cw:5 * cw], in0=p5s[c][:, 0:cw], scalar=col("e5"),
+                                           in1=z[:, 0:cw], op0=ALU.add, op1=ALU.mult)
+            if fc > 0:
+                ts(tb[:, 0:fc], z[:, 0:fc], col("c11"))
 
         def quantise(c):
+            cw, nw = SIZES[c] * I, SIZES[c] * P
             cod = work.tile([P, DEG * NW], U32, name="cod", align_bytes=64)
             scl = work.tile([P, DEG * NW], U8, name="scl", align_bytes=64)
             for d0, d1 in ((2, 4), (4, 5), (0, 2)):
-                nc.vector.quantize_mx(out=cod[:, d0 * NW:d1 * NW].bitcast(FP8X4), scales=scl[:, d0 * NW:d1 * NW],
-                                      in_=tbs[c][:, d0 * CW:d1 * CW])
+                nc.vector.quantize_mx(out=cod[:, d0 * nw:d1 * nw].bitcast(FP8X4), scales=scl[:, d0 * nw:d1 * nw],
+                                      in_=tbs[c][:, d0 * cw:d1 * cw])
             cods[c], scls[c] = cod, scl
 
         def mx(c):
+            nw = SIZES[c] * P
             yt = psum.tile([P, NW], F32, name="yt", tag="yt")
             order = (2, 3, 4, 0, 1)
             for n, d in enumerate(order):
                 nc.tensor.matmul_mx(
-                    out=yt[:],
+                    out=yt[:, 0:nw],
                     lhsT=ccod[:, d * O:(d + 1) * O].bitcast(FP8X4), lhsT_scale=cscl[:, d * O:(d + 1) * O],
-                    rhs=cods[c][:, d * NW:(d + 1) * NW].bitcast(FP8X4), rhs_scale=scls[c][:, d * NW:(d + 1) * NW],
+                    rhs=cods[c][:, d * nw:(d + 1) * nw].bitcast(FP8X4), rhs_scale=scls[c][:, d * nw:(d + 1) * nw],
                     start=(n == 0), stop=(n == DEG - 1))
             yt_ps[c] = yt
 
         def evacuate(c):
-            yts = small.tile([P, NW], F32, name="yts")
-            nc.scalar.activation(out=yts[:], in_=yt_ps[c][:], func=ACT.Identity, bias=y0[:, 0:1])
+            yts = stat.tile([P, NW], F32, name="yts")
+            nw = SIZES[c] * P
+            nc.scalar.activation(out=yts[:, 0:nw], in_=yt_ps[c][:, 0:nw], func=ACT.Identity, bias=y0[:, 0:1])
             ytss[c] = yts
 
         def y_transposes(c):
             yst = psum.tile([P, NW], F32, name="yst", tag="yst")
-            for j in range(G):
+            for j in range(SIZES[c]):
                 nc.tensor.transpose(yst[:, j * O:(j + 1) * O], ytss[c][:, j * P:(j + 1) * P], ident[:])
             ysts[c] = yst
 
         def stats(c):
-            st = small.tile([P, G, 6], F32, name="st")
-            mv = small.tile([P, G, 2], F32, name="mv")
-            for j in range(G):
+            g = SIZES[c]
+            st = stat.tile([P, G, 6], F32, name="st")
+            for j in range(g):
                 nc.vector.bn_stats(out=st[:, j, :], in_=ysts[c][:, j * O:(j + 1) * O])
-            for j in range(G):
-                nc.vector.bn_aggr(out=mv[:, j, :], in_=st[:, j, :])
-            ve = small.tile([P, G], F32, name="ve")
-            ts(ve[:], mv[:, :, 1], LN_EPS, op0=ALU.add)
-            rstd = small.tile([P, G], F32, name="rstd")
-            nc.gpsimd.tensor_tensor(out=rstd[:], in0=ve[:], in1=mhalf[:], op=ALU.pow)
+            gd = stat.tile([P, G], F32, name="gd")
+            nc.gpsimd.tensor_tensor(out=gd[:, 0:g], in0=st[:, 0:g, 1], in1=st[:, 0:g, 4], op=ALU.subtract)
+            gs = stat.tile([P, G], F32, name="gs")
+            nc.gpsimd.tensor_tensor(out=gs[:, 0:g], in0=st[:, 0:g, 2], in1=st[:, 0:g, 5], op=ALU.add)
+            gdd = stat.tile([P, G], F32, name="gdd")
+            nc.gpsimd.tensor_tensor(out=gdd[:, 0:g], in0=gd[:, 0:g], in1=gd[:, 0:g], op=ALU.mult)
+            gs2 = stat.tile([P, G], F32, name="gs2")
+            nc.gpsimd.tensor_scalar(out=gs2[:, 0:g], in0=gs[:, 0:g], scalar1=4.0 / O, scalar2=4.0 * LN_EPS,
+                                    op0=ALU.mult, op1=ALU.add)
+            gu = stat.tile([P, G], F32, name="gu")
+            nc.gpsimd.tensor_tensor(out=gu[:, 0:g], in0=gdd[:, 0:g], in1=gs2[:, 0:g], op=ALU.add)
+            rstd = stat.tile([P, G], F32, name="rstd")
+            nc.gpsimd.tensor_tensor(out=rstd[:, 0:g], in0=gu[:, 0:g], in1=mhalf[:, 0:g], op=ALU.pow)
             rstds[c] = rstd
 
         def centre(c):
             ycg = psum.tile([P, NW], F32, name="ycg", tag="ycg")
-            for j in range(G):
+            for j in range(SIZES[c]):
                 nc.tensor.matmul(out=ycg[:, j * O:(j + 1) * O], lhsT=ytss[c][:, j * P:(j + 1) * P], rhs=ceng[:],
                                  start=True, stop=True)
             ycgs[c] = ycg
 
-        def final(c):
-            osb = small.tile([P, G * O], F32, name="osb")
-            for j in range(G):
+        def final(c, j0, j1):
+            if j0 == 0:
+                osbs[c] = small.tile([P, G * O], F32, name="osb")
+            osb = osbs[c]
+            for j in range(j0, j1):
                 nc.vector.scalar_tensor_tensor(out=osb[:, j * O:(j + 1) * O], in0=ycgs[c][:, j * O:(j + 1) * O],
                                                scalar=rstds[c][:, j:j + 1], in1=b_b[:], op0=ALU.mult, op1=ALU.add)
-            nc.sync.dma_start(out=out_v[:, c * G * O:(c + 1) * G * O], in_=osb[:])
+            if j1 == SIZES[c]:
+                nc.sync.dma_start(out=out_v[:, STARTS[c] * O:(STARTS[c] + SIZES[c]) * O], in_=osb[:, 0:SIZES[c] * O])
 
         craw4 = craw[:].rearrange("p (t o d) -> p t o d", t=4, o=O, d=6)
         c0 = const.tile([P, 4 * O], BF16, name="c0")
@@ -275,34 +302,40 @@ def tile_gottliebkanlayer_t_kernel(tc, x, alpha, coeffs, ln_weight, ln_bias, out
                 nc.tensor.matmul(out=ps0[:], lhsT=c0[:, t * O:(t + 1) * O], rhs=ones[:], start=(t == 0),
                                  stop=(t == 3))
             nc.vector.tensor_copy(out=y0[:], in_=ps0[:, 0:1])
-            ts(cen[:], ident[:], -1.0 / O, op0=ALU.add)
+            ts(cen[:], ident[:], -1.0 / O, 2.0, ALU.add, ALU.mult)
             nc.vector.tensor_tensor(out=ceng[:], in0=cen[:], in1=g_b[:], op=ALU.mult)
 
-        x_transposes(0)
-        for k in range(NCH + 2):
+        for c in range(2):
+            x_transposes(c)
+            sigmoid(c)
+        lag = 4
+        for k in range(NCH + lag):
             if k < NCH:
-                sigmoid(k)
-                if k + 1 < NCH:
-                    x_transposes(k + 1)
-                if k + 4 < NCH:
-                    load_x(k + 4)
-            if 0 <= k - 2:
-                centre(k - 2)
+                square_w3(k)
+            if 0 <= k - 2 < NCH:
+                evacuate(k - 2)
+            if k < NCH:
+                squares_p4_p5(k)
+            if 1 <= k and k + 1 < NCH:
+                x_transposes(k + 1)
+            if k + 4 < NCH:
+                load_x(k + 4)
+            if 0 <= k - 2 < NCH:
+                y_transposes(k - 2)
+            if 0 <= k - lag:
+                centre(k - lag)
             if 0 <= k - 1 < NCH:
                 mx(k - 1)
-            if k < NCH:
-                squares(k)
-            if 0 <= k - 1 < NCH:
-                evacuate(k - 1)
-                y_transposes(k - 1)
+            if 1 <= k and k + 1 < NCH:
+                sigmoid(k + 1)
             if k < NCH:
                 t1_scalar(k)
                 basis(k)
             if k == 0:
                 coefficient_work()
-            if 0 <= k - 1 < NCH:
-                stats(k - 1)
-            if 0 <= k - 2:
-                final(k - 2)
+            if 0 <= k - 2 < NCH:
+                stats(k - 2)
+            if 0 <= k - lag:
+                final(k - lag, 0, SIZES[k - lag])
             if k < NCH:
                 quantise(k)

@@ -24,7 +24,7 @@ NW = CW // 4
 LN_EPS = 1e-5
 FLOPS = 2 * B * I * O * DEG
 
-T1_VECTOR_COLS = tuple(g * I if c < 2 else (0 if c >= NCH - 3 else 256 * g // G) for c, g in enumerate(SIZES))
+T1_VECTOR_COLS = tuple(g * I if c < 2 else (0 if c >= NCH - 3 else 512 * g // G) for c, g in enumerate(SIZES))
 
 
 def tile_gottliebkanlayer_t_kernel(tc, x, alpha, coeffs, ln_weight, ln_bias, out):
@@ -36,7 +36,6 @@ def tile_gottliebkanlayer_t_kernel(tc, x, alpha, coeffs, ln_weight, ln_bias, out
         xin = ctx.enter_context(tc.tile_pool(name="xin", bufs=4))
         work = ctx.enter_context(tc.tile_pool(name="work", bufs=2))
         small = ctx.enter_context(tc.tile_pool(name="small", bufs=3))
-        stat = ctx.enter_context(tc.tile_pool(name="stat", bufs=5))
         psum = ctx.enter_context(tc.psum_pool(name="psum", bufs=2))
         ctx.enter_context(tc.manual_schedule())
 
@@ -228,7 +227,7 @@ def tile_gottliebkanlayer_t_kernel(tc, x, alpha, coeffs, ln_weight, ln_bias, out
             yt_ps[c] = yt
 
         def evacuate(c):
-            yts = stat.tile([P, NW], F32, name="yts")
+            yts = small.tile([P, NW], F32, name="yts")
             nw = SIZES[c] * P
             nc.scalar.activation(out=yts[:, 0:nw], in_=yt_ps[c][:, 0:nw], func=ACT.Identity, bias=y0[:, 0:1])
             ytss[c] = yts
@@ -240,23 +239,20 @@ def tile_gottliebkanlayer_t_kernel(tc, x, alpha, coeffs, ln_weight, ln_bias, out
             ysts[c] = yst
 
         def stats(c):
-            g = SIZES[c]
-            st = stat.tile([P, G, 6], F32, name="st")
-            for j in range(g):
+            st = small.tile([P, G, 6], F32, name="st")
+            mv = small.tile([P, G, 2], F32, name="mv")
+            for j in range(SIZES[c]):
                 nc.vector.bn_stats(out=st[:, j, :], in_=ysts[c][:, j * O:(j + 1) * O])
-            gd = stat.tile([P, G], F32, name="gd")
-            nc.gpsimd.tensor_tensor(out=gd[:, 0:g], in0=st[:, 0:g, 1], in1=st[:, 0:g, 4], op=ALU.subtract)
-            gs = stat.tile([P, G], F32, name="gs")
-            nc.gpsimd.tensor_tensor(out=gs[:, 0:g], in0=st[:, 0:g, 2], in1=st[:, 0:g, 5], op=ALU.add)
-            gdd = stat.tile([P, G], F32, name="gdd")
-            nc.gpsimd.tensor_tensor(out=gdd[:, 0:g], in0=gd[:, 0:g], in1=gd[:, 0:g], op=ALU.mult)
-            gs2 = stat.tile([P, G], F32, name="gs2")
-            nc.gpsimd.tensor_scalar(out=gs2[:, 0:g], in0=gs[:, 0:g], scalar1=4.0 / O, scalar2=4.0 * LN_EPS,
-                                    op0=ALU.mult, op1=ALU.add)
-            gu = stat.tile([P, G], F32, name="gu")
-            nc.gpsimd.tensor_tensor(out=gu[:, 0:g], in0=gdd[:, 0:g], in1=gs2[:, 0:g], op=ALU.add)
-            rstd = stat.tile([P, G], F32, name="rstd")
-            nc.gpsimd.tensor_tensor(out=rstd[:, 0:g], in0=gu[:, 0:g], in1=mhalf[:, 0:g], op=ALU.pow)
+            for j in range(SIZES[c]):
+                nc.vector.bn_aggr(out=mv[:, j, :], in_=st[:, j, :])
+            mvs[c] = mv
+
+        def rstd_of(c):
+            ve = small.tile([P, G], F32, name="ve")
+            g = SIZES[c]
+            ts(ve[:, 0:g], mvs[c][:, 0:g, 1], LN_EPS, op0=ALU.add)
+            rstd = small.tile([P, G], F32, name="rstd")
+            nc.gpsimd.tensor_tensor(out=rstd[:, 0:g], in0=ve[:, 0:g], in1=mhalf[:, 0:g], op=ALU.pow)
             rstds[c] = rstd
 
         def centre(c):
@@ -302,14 +298,13 @@ def tile_gottliebkanlayer_t_kernel(tc, x, alpha, coeffs, ln_weight, ln_bias, out
                 nc.tensor.matmul(out=ps0[:], lhsT=c0[:, t * O:(t + 1) * O], rhs=ones[:], start=(t == 0),
                                  stop=(t == 3))
             nc.vector.tensor_copy(out=y0[:], in_=ps0[:, 0:1])
-            ts(cen[:], ident[:], -1.0 / O, 2.0, ALU.add, ALU.mult)
+            ts(cen[:], ident[:], -1.0 / O, op0=ALU.add)
             nc.vector.tensor_tensor(out=ceng[:], in0=cen[:], in1=g_b[:], op=ALU.mult)
 
         for c in range(2):
             x_transposes(c)
             sigmoid(c)
-        lag = 4
-        for k in range(NCH + lag):
+        for k in range(NCH + 3):
             if k < NCH:
                 square_w3(k)
             if 0 <= k - 2 < NCH:
@@ -322,8 +317,8 @@ def tile_gottliebkanlayer_t_kernel(tc, x, alpha, coeffs, ln_weight, ln_bias, out
                 load_x(k + 4)
             if 0 <= k - 2 < NCH:
                 y_transposes(k - 2)
-            if 0 <= k - lag:
-                centre(k - lag)
+            if 0 <= k - 3:
+                centre(k - 3)
             if 0 <= k - 1 < NCH:
                 mx(k - 1)
             if 1 <= k and k + 1 < NCH:
@@ -335,7 +330,11 @@ def tile_gottliebkanlayer_t_kernel(tc, x, alpha, coeffs, ln_weight, ln_bias, out
                 coefficient_work()
             if 0 <= k - 2 < NCH:
                 stats(k - 2)
-            if 0 <= k - lag:
-                final(k - lag, 0, SIZES[k - lag])
+            if 0 <= k - 3:
+                final(k - 3, 0, 1)
+            if 0 <= k - 2 < NCH:
+                rstd_of(k - 2)
+            if 0 <= k - 3 and SIZES[k - 3] > 1:
+                final(k - 3, 1, SIZES[k - 3])
             if k < NCH:
                 quantise(k)

@@ -24,7 +24,7 @@ NW = CW // 4
 LN_EPS = 1e-5
 FLOPS = 2 * B * I * O * DEG
 
-T1_VECTOR_COLS = tuple(g * I if c < 2 else (0 if c >= NCH - 3 else 512 * g // G) for c, g in enumerate(SIZES))
+T1_VECTOR_COLS = tuple(g * I if c < 2 else 0 for c, g in enumerate(SIZES))
 
 
 def tile_gottliebkanlayer_t_kernel(tc, x, alpha, coeffs, ln_weight, ln_bias, out):
@@ -36,6 +36,7 @@ def tile_gottliebkanlayer_t_kernel(tc, x, alpha, coeffs, ln_weight, ln_bias, out
         xin = ctx.enter_context(tc.tile_pool(name="xin", bufs=4))
         work = ctx.enter_context(tc.tile_pool(name="work", bufs=2))
         small = ctx.enter_context(tc.tile_pool(name="small", bufs=3))
+        stat = ctx.enter_context(tc.tile_pool(name="stat", bufs=5))
         psum = ctx.enter_context(tc.psum_pool(name="psum", bufs=2))
         ctx.enter_context(tc.manual_schedule())
 
@@ -227,7 +228,7 @@ def tile_gottliebkanlayer_t_kernel(tc, x, alpha, coeffs, ln_weight, ln_bias, out
             yt_ps[c] = yt
 
         def evacuate(c):
-            yts = small.tile([P, NW], F32, name="yts")
+            yts = stat.tile([P, NW], F32, name="yts")
             nw = SIZES[c] * P
             nc.scalar.activation(out=yts[:, 0:nw], in_=yt_ps[c][:, 0:nw], func=ACT.Identity, bias=y0[:, 0:1])
             ytss[c] = yts
@@ -239,8 +240,8 @@ def tile_gottliebkanlayer_t_kernel(tc, x, alpha, coeffs, ln_weight, ln_bias, out
             ysts[c] = yst
 
         def stats(c):
-            st = small.tile([P, G, 6], F32, name="st")
-            mv = small.tile([P, G, 2], F32, name="mv")
+            st = stat.tile([P, G, 6], F32, name="st")
+            mv = stat.tile([P, G, 2], F32, name="mv")
             for j in range(SIZES[c]):
                 nc.vector.bn_stats(out=st[:, j, :], in_=ysts[c][:, j * O:(j + 1) * O])
             for j in range(SIZES[c]):
@@ -248,10 +249,10 @@ def tile_gottliebkanlayer_t_kernel(tc, x, alpha, coeffs, ln_weight, ln_bias, out
             mvs[c] = mv
 
         def rstd_of(c):
-            ve = small.tile([P, G], F32, name="ve")
+            ve = stat.tile([P, G], F32, name="ve")
             g = SIZES[c]
             ts(ve[:, 0:g], mvs[c][:, 0:g, 1], LN_EPS, op0=ALU.add)
-            rstd = small.tile([P, G], F32, name="rstd")
+            rstd = stat.tile([P, G], F32, name="rstd")
             nc.gpsimd.tensor_tensor(out=rstd[:, 0:g], in0=ve[:, 0:g], in1=mhalf[:, 0:g], op=ALU.pow)
             rstds[c] = rstd
 
@@ -304,7 +305,7 @@ def tile_gottliebkanlayer_t_kernel(tc, x, alpha, coeffs, ln_weight, ln_bias, out
         for c in range(2):
             x_transposes(c)
             sigmoid(c)
-        for k in range(NCH + 3):
+        for k in range(NCH + 4):
             if k < NCH:
                 square_w3(k)
             if 0 <= k - 2 < NCH:
@@ -317,8 +318,8 @@ def tile_gottliebkanlayer_t_kernel(tc, x, alpha, coeffs, ln_weight, ln_bias, out
                 load_x(k + 4)
             if 0 <= k - 2 < NCH:
                 y_transposes(k - 2)
-            if 0 <= k - 3:
-                centre(k - 3)
+            if 0 <= k - 4:
+                centre(k - 4)
             if 0 <= k - 1 < NCH:
                 mx(k - 1)
             if 1 <= k and k + 1 < NCH:
@@ -328,13 +329,11 @@ def tile_gottliebkanlayer_t_kernel(tc, x, alpha, coeffs, ln_weight, ln_bias, out
                 basis(k)
             if k == 0:
                 coefficient_work()
+            if 0 <= k - 3 < NCH:
+                rstd_of(k - 3)
             if 0 <= k - 2 < NCH:
                 stats(k - 2)
-            if 0 <= k - 3:
-                final(k - 3, 0, 1)
-            if 0 <= k - 2 < NCH:
-                rstd_of(k - 2)
-            if 0 <= k - 3 and SIZES[k - 3] > 1:
-                final(k - 3, 1, SIZES[k - 3])
+            if 0 <= k - 4:
+                final(k - 4, 0, SIZES[k - 4])
             if k < NCH:
                 quantise(k)

@@ -24,7 +24,7 @@ NW = CW // 4
 LN_EPS = 1e-5
 FLOPS = 2 * B * I * O * DEG
 
-T1_VECTOR_COLS = tuple(g * I if c < 2 else 0 for c, g in enumerate(SIZES))
+T1_VECTOR_COLS = tuple(g * I if c < 2 else (0 if c >= NCH - 3 else 256 * g // G) for c, g in enumerate(SIZES))
 
 
 def tile_gottliebkanlayer_t_kernel(tc, x, alpha, coeffs, ln_weight, ln_bias, out):
@@ -63,7 +63,7 @@ def tile_gottliebkanlayer_t_kernel(tc, x, alpha, coeffs, ln_weight, ln_bias, out
 
         cst0 = const.tile([P, 9], F32, name="cst0")
         nc.vector.memset(cst0[:], 2.0)
-        for k, v in ((0, 0.0), (2, 6.0), (3, 1.0), (6, 3.0), (7, 4.0), (8, 8.0)):
+        for k, v in ((0, 3.0), (1, 0.0), (3, 6.0), (4, 4.0), (5, 1.0), (8, 8.0)):
             nc.vector.memset(cst0[:, k:k + 1], v)
         floors = const.tile([P, 3], F32, name="floors")
         powe = const.tile([P, 3], F32, name="powe")
@@ -77,10 +77,10 @@ def tile_gottliebkanlayer_t_kernel(tc, x, alpha, coeffs, ln_weight, ln_bias, out
         ident = const.tile([P, P], F32, name="ident")
         make_identity(nc, ident[:])
 
-        names = ("a0", "a2", "a6", "a1", "a2b", "a2c", "a3", "a4", "a8", "p01", "a2sq", "c40", "c42", "c31", "c33",
-                 "c44", "c55", "c51", "c53", "h3", "h4", "h5", "sg3", "sg4", "sg5", "aa3", "aa4", "aa5", "ab3", "ab4",
-                 "ab5", "r3", "r4", "r5", "v3", "t1", "u0", "u1", "w0", "w1", "m2", "e3", "x1", "b4", "yy", "k4", "mm",
-                 "m4", "t5", "b5", "nt", "e5", "s5", "c11", "c20")
+        names = ("a3", "a0", "a2", "a6", "a4", "a1", "a2b", "a2c", "a8", "a34", "p01", "a2sq", "c40", "c42", "c31", "c33",
+                 "c44", "c55", "c51", "c53", "f1", "f2", "f3", "c33s", "h3", "h4", "h5", "sg3", "sg4", "sg5", "aa3",
+                 "aa4", "aa5", "ab3", "ab4", "ab5", "r3", "r4", "r5", "v3", "t1", "u0", "u1", "w0", "w1", "m2", "e3",
+                 "x1", "b4", "yy", "k4", "mm", "m4", "t5", "b5", "nt", "e5", "s5", "c11", "c20")
         sc = const.tile([P, len(names)], F32, name="sc")
         idx = dict((n, k) for k, n in enumerate(names))
 
@@ -96,41 +96,43 @@ def tile_gottliebkanlayer_t_kernel(tc, x, alpha, coeffs, ln_weight, ln_bias, out
         def stt(o, i0, s, i1, op0, op1):
             nc.vector.scalar_tensor_tensor(out=o, in0=i0, scalar=s, in1=i1, op0=op0, op1=op1)
 
-        ts(col("a0", 9), cst0[:], a_bf[:, 0:1], op0=ALU.add)
-        nc.vector.tensor_tensor(out=col("p01", 3), in0=col("a0", 3), in1=col("a1", 3), op=ALU.mult)
-        stt(col("c33"), col("p01"), 8.0, col("a2"), ALU.mult, ALU.mult)
-        ts(col("c44"), col("c33"), col("a3"), 2.0)
-        ts(col("c55"), col("c44"), col("a4"), 2.0)
+        nc.vector.memset(col("f1"), 1.0)
+        ts(col("a3", 9), cst0[:], a_bf[:, 0:1], op0=ALU.add)
+        nc.vector.tensor_tensor(out=col("a34", 4), in0=col("a3", 4), in1=col("a4", 4), op=ALU.mult)
+        stt(col("c33s"), col("p01"), 8.0, col("a2"), ALU.mult, ALU.mult)
+        ts(col("f2"), col("a3"), 2.0)
+        ts(col("f3"), col("a34"), 4.0)
+        ts(col("c31"), col("a2sq"), -4.0, 8.0, ALU.mult, ALU.add)
+        ts(col("c33", 3), col("f1", 3), col("c33s"))
+        ts(col("v3"), col("p01"), col("a6"), -4.0)
+        ts(col("t1"), col("c31"), col("a3"), 2.0)
+        ts(col("c11"), col("a0"), 2.0)
+        stt(col("aa3", 3), col("c33", 3), -1.0, col("c33", 3), ALU.mult, ALU.max)
         ts(col("h3", 3), col("c33", 3), 0.0, 0.5, ALU.is_ge, ALU.subtract)
-        stt(col("aa3", 3), col("c33", 3), 2.0, col("h3", 3), ALU.mult, ALU.mult)
+        nc.vector.tensor_tensor(out=col("c42"), in0=col("t1"), in1=col("v3"), op=ALU.add)
+        ts(col("c20"), col("a2"), -1.0)
+        c20 = col("c20")
         nc.vector.tensor_tensor(out=col("ab3", 3), in0=col("aa3", 3), in1=floors[:], op=ALU.max)
         gp = const.tile([P, 3], F32, name="gp")
         nc.gpsimd.tensor_tensor(out=gp[:], in0=col("ab3", 3), in1=powe[:], op=ALU.pow)
         s3 = gp[:, 0:1]
         ir5 = gp[:, 2:3]
-        ts(col("c11"), col("a0"), 2.0)
-        ts(col("c20"), col("a2"), -1.0)
-        c20 = col("c20")
         ts(col("sg3", 3), col("h3", 3), 2.0)
-        nc.vector.reciprocal(out=col("r3", 3), in_=col("ab3", 3))
-        ts(col("c31"), col("a2sq"), -4.0, 8.0, ALU.mult, ALU.add)
-        ts(col("v3"), col("p01"), col("a6"), -4.0)
-        ts(col("t1"), col("c31"), col("a3"), 2.0)
-        nc.vector.tensor_tensor(out=col("c42"), in0=col("t1"), in1=col("v3"), op=ALU.add)
-        ts(col("m2"), col("p01"), col("r3"), 4.0)
-        ts(col("e3"), col("c31"), col("sg3"))
-        ts(col("x1"), col("c42"), col("r4"), 0.5)
-        ts(col("b4"), col("x1"), col("ab3"), col("sg4"))
-        ts(col("u0", 2), col("c40", 2), col("a4"), 2.0)
         ts(col("w0", 2), col("c31", 2), col("a8"))
+        ts(col("u0", 2), col("c40", 2), col("a4"), 2.0)
+        nc.vector.reciprocal(out=col("r3", 3), in_=col("ab3", 3))
+        ts(col("e3"), col("c31"), col("sg3"))
         nc.vector.tensor_tensor(out=col("c51", 2), in0=col("u0", 2), in1=col("w0", 2), op=ALU.subtract)
+        ts(col("x1"), col("c42"), col("r4"), 0.5)
+        ts(col("m2"), col("p01"), col("r3"), 4.0)
+        ts(col("mm"), col("r3"), col("r3"), col("ab4"))
+        ts(col("b4"), col("x1"), col("ab3"), col("sg4"))
+        ts(col("yy"), col("x1"), col("c42"), col("sg4"))
+        ts(col("m4"), col("mm"), col("sg4"))
+        stt(col("k4"), col("yy"), -0.5, col("c40"), ALU.mult, ALU.add)
         ts(col("t5"), col("c53"), ir5, 0.5)
         ts(col("s5"), col("ab5"), ir5, col("r3"))
         ts(col("b5"), col("t5"), col("sg5"))
-        ts(col("yy"), col("x1"), col("c42"), col("sg4"))
-        stt(col("k4"), col("yy"), -0.5, col("c40"), ALU.mult, ALU.add)
-        ts(col("mm"), col("r3"), col("r3"), col("ab4"))
-        ts(col("m4"), col("mm"), col("sg4"))
         ts(col("nt"), col("t5"), col("t5"), -1.0)
         stt(col("e5"), col("c51"), col("sg5"), col("nt"), ALU.mult, ALU.add)
 

from contextlib import ExitStack

import concourse.mybir as mybir
from concourse.masks import make_identity

F32 = mybir.dt.float32
BF16 = mybir.dt.bfloat16
U32 = mybir.dt.uint32
U8 = mybir.dt.uint8
FP8X4 = mybir.dt.float8_e4m3fn_x4
ALU = mybir.AluOpType
ACT = mybir.ActivationFunctionType

P = 128
B, I, O, DEG = 8192, 512, 128, 5
NT = B // P
G = 4
SIZES = (2, 2) + (4,) * 14 + (2, 1, 1)
NCH = len(SIZES)
STARTS = tuple(sum(SIZES[:c]) for c in range(NCH))
assert sum(SIZES) == NT
CW = G * I
NW = CW // 4
LN_EPS = 1e-5
FLOPS = 2 * B * I * O * DEG

T1_VECTOR_COLS = tuple(g * I if c < 2 else (0 if c >= NCH - 3 else 256 * g // G) for c, g in enumerate(SIZES))


def tile_gottliebkanlayer_t_kernel(tc, x, alpha, coeffs, ln_weight, ln_bias, out):
    nc = tc.nc
    x_v = x.rearrange("(p t) i -> p (t i)", t=NT)
    out_v = out.rearrange("(p t) o -> p (t o)", t=NT)
    with ExitStack() as ctx:
        const = ctx.enter_context(tc.tile_pool(name="const", bufs=1))
        xin = ctx.enter_context(tc.tile_pool(name="xin", bufs=4))
        work = ctx.enter_context(tc.tile_pool(name="work", bufs=2))
        small = ctx.enter_context(tc.tile_pool(name="small", bufs=3))
        stat = ctx.enter_context(tc.tile_pool(name="stat", bufs=5))
        psum = ctx.enter_context(tc.psum_pool(name="psum", bufs=2))
        ctx.enter_context(tc.manual_schedule())

        x_tiles = {}

        def load_x(c):
            x_sb = xin.tile([P, CW], BF16, name="x_sb")
            nc.sync.dma_start(out=x_sb[:, 0:SIZES[c] * I], in_=x_v[:, STARTS[c] * I:(STARTS[c] + SIZES[c]) * I])
            x_tiles[c] = x_sb

        for c in range(4):
            load_x(c)
        a_bf = const.tile([P, 1], BF16, name="a_bf")
        nc.scalar.dma_start(out=a_bf[:], in_=alpha.partition_broadcast(P))
        craw = const.tile([P, 4 * O * 6], BF16, name="craw")
        nc.scalar.dma_start(
            out=craw[:].rearrange("p (u r) -> p u r", u=2),
            in_=coeffs.rearrange("(u q e) o d -> q u (e o d)", u=2, e=2),
        )
        g_b = const.tile([P, O], BF16, name="g_b")
        nc.scalar.dma_start(out=g_b[:], in_=ln_weight.partition_broadcast(P))
        b_b = const.tile([P, O], BF16, name="b_b")
        nc.scalar.dma_start(out=b_b[:], in_=ln_bias.partition_broadcast(P))

        cst0 = const.tile([P, 9], F32, name="cst0")
        nc.vector.memset(cst0[:], 2.0)
        for k, v in ((0, 3.0), (1, 0.0), (3, 6.0), (4, 4.0), (5, 1.0), (8, 8.0)):
            nc.vector.memset(cst0[:, k:k + 1], v)
        floors = const.tile([P, 3], F32, name="floors")
        powe = const.tile([P, 3], F32, name="powe")
        for k, (lo, ex) in enumerate(((1e-4, 0.5), (6e-3, 1.0), (5e-2, -0.5))):
            nc.vector.memset(floors[:, k:k + 1], lo)
            nc.vector.memset(powe[:, k:k + 1], ex)
        mhalf = const.tile([P, G], F32, name="mhalf")
        nc.vector.memset(mhalf[:], -0.5)
        ones = const.tile([P, 64], BF16, name="ones")
        nc.vector.memset(ones[:], 1.0)
        ident = const.tile([P, P], F32, name="ident")
        make_identity(nc, ident[:])

        names = ("a3", "a0", "a2", "a6", "a4", "a1", "a2b", "a2c", "a8", "a34", "p01", "a2sq", "c40", "c42", "c31", "c33",
                 "c44", "c55", "c51", "c53", "f1", "f2", "f3", "c33s", "h3", "h4", "h5", "sg3", "sg4", "sg5", "aa3",
                 "aa4", "aa5", "ab3", "ab4", "ab5", "r3", "r4", "r5", "v3", "t1", "u0", "u1", "w0", "w1", "m2", "e3",
                 "x1", "b4", "yy", "k4", "mm", "m4", "t5", "b5", "nt", "e5", "s5", "c11", "c20")
        sc = const.tile([P, len(names)], F32, name="sc")
        idx = dict((n, k) for k, n in enumerate(names))

        def col(n, w=1):
            return sc[:, idx[n]:idx[n] + w]

        def ts(o, i, s1, s2=None, op0=ALU.mult, op1=ALU.mult):
            if s2 is None:
                nc.vector.tensor_scalar(out=o, in0=i, scalar1=s1, scalar2=None, op0=op0)
            else:
                nc.vector.tensor_scalar(out=o, in0=i, scalar1=s1, scalar2=s2, op0=op0, op1=op1)

        def stt(o, i0, s, i1, op0, op1):
            nc.vector.scalar_tensor_tensor(out=o, in0=i0, scalar=s, in1=i1, op0=op0, op1=op1)

        nc.vector.memset(col("f1"), 1.0)
        ts(col("a3", 9), cst0[:], a_bf[:, 0:1], op0=ALU.add)
        nc.vector.tensor_tensor(out=col("a34", 4), in0=col("a3", 4), in1=col("a4", 4), op=ALU.mult)
        stt(col("c33s"), col("p01"), 8.0, col("a2"), ALU.mult, ALU.mult)
        ts(col("f2"), col("a3"), 2.0)
        ts(col("f3"), col("a34"), 4.0)
        ts(col("c31"), col("a2sq"), -4.0, 8.0, ALU.mult, ALU.add)
        ts(col("c33", 3), col("f1", 3), col("c33s"))
        ts(col("v3"), col("p01"), col("a6"), -4.0)
        ts(col("t1"), col("c31"), col("a3"), 2.0)
        ts(col("c11"), col("a0"), 2.0)
        stt(col("aa3", 3), col("c33", 3), -1.0, col("c33", 3), ALU.mult, ALU.max)
        ts(col("h3", 3), col("c33", 3), 0.0, 0.5, ALU.is_ge, ALU.subtract)
        nc.vector.tensor_tensor(out=col("c42"), in0=col("t1"), in1=col("v3"), op=ALU.add)
        ts(col("c20"), col("a2"), -1.0)
        c20 = col("c20")
        nc.vector.tensor_tensor(out=col("ab3", 3), in0=col("aa3", 3), in1=floors[:], op=ALU.max)
        gp = const.tile([P, 3], F32, name="gp")
        nc.gpsimd.tensor_tensor(out=gp[:], in0=col("ab3", 3), in1=powe[:], op=ALU.pow)
        s3 = gp[:, 0:1]
        ir5 = gp[:, 2:3]
        ts(col("sg3", 3), col("h3", 3), 2.0)
        ts(col("w0", 2), col("c31", 2), col("a8"))
        ts(col("u0", 2), col("c40", 2), col("a4"), 2.0)
        nc.vector.reciprocal(out=col("r3", 3), in_=col("ab3", 3))
        ts(col("e3"), col("c31"), col("sg3"))
        nc.vector.tensor_tensor(out=col("c51", 2), in0=col("u0", 2), in1=col("w0", 2), op=ALU.subtract)
        ts(col("x1"), col("c42"), col("r4"), 0.5)
        ts(col("m2"), col("p01"), col("r3"), 4.0)
        ts(col("mm"), col("r3"), col("r3"), col("ab4"))
        ts(col("b4"), col("x1"), col("ab3"), col("sg4"))
        ts(col("yy"), col("x1"), col("c42"), col("sg4"))
        ts(col("m4"), col("mm"), col("sg4"))
        stt(col("k4"), col("yy"), -0.5, col("c40"), ALU.mult, ALU.add)
        ts(col("t5"), col("c53"), ir5, 0.5)
        ts(col("s5"), col("ab5"), ir5, col("r3"))
        ts(col("b5"), col("t5"), col("sg5"))
        ts(col("nt"), col("t5"), col("t5"), -1.0)
        stt(col("e5"), col("c51"), col("sg5"), col("nt"), ALU.mult, ALU.add)

        xts = {}
        zs = {}
        w3s = {}
        p4s = {}
        p5s = {}
        tbs = {}
        cods = {}
        scls = {}
        yt_ps = {}
        ytss = {}
        ysts = {}
        rstds = {}
        ycgs = {}
        mvs = {}
        osbs = {}

        def x_transposes(c):
            xw = x_tiles[c][:].bitcast(F32)
            for h in range((SIZES[c] + 1) // 2):
                m = min(2, SIZES[c] - 2 * h)
                xt = psum.tile([P, 512], F32, name="xt", tag="xt")
                for j2 in range(m):
                    for u in range(2):
                        nc.tensor.transpose(
                            xt[:, (u * m + j2) * P:(u * m + j2 + 1) * P],
                            xw[:, (2 * h + j2) * 256 + u * P:(2 * h + j2) * 256 + (u + 1) * P],
                            ident[:])
                xts[(c, h)] = xt

        def sigmoid(c):
            z = work.tile([P, CW], F32, name="z")
            for h in range((SIZES[c] + 1) // 2):
                m = min(2, SIZES[c] - 2 * h)
                nc.scalar.activation(
                    out=z[:, h * 1024:h * 1024 + m * I].rearrange("p (n u e) -> p n u e", u=2, e=2),
                    in_=xts[(c, h)][:].bitcast(BF16)[:, 0:4 * m * P].rearrange("p (u n e) -> p n u e", u=2, e=2),
                    func=ACT.Sigmoid)
            zs[c] = z

        def square_w3(c):
            w3 = work.tile([P, CW], F32, name="w3")
            cw = SIZES[c] * I
            nc.scalar.activation(out=w3[:, 0:cw], in_=zs[c][:, 0:cw], func=ACT.Square, scale=s3)
            w3s[c] = w3

        def squares_p4_p5(c):
            w3 = w3s[c]
            cw = SIZES[c] * I
            p4 = work.tile([P, CW], F32, name="p4")
            nc.scalar.activation(out=p4[:, 0:cw], in_=w3[:, 0:cw], func=ACT.Square, bias=col("b4"))
            p5 = work.tile([P, CW], F32, name="p5")
            nc.scalar.activation(out=p5[:, 0:cw], in_=w3[:, 0:cw], func=ACT.Square, scale=col("s5"), bias=col("b5"))
            p4s[c], p5s[c] = p4, p5
            tbs[c] = work.tile([P, DEG * CW], BF16, name="tb", align_bytes=64)

        def t1_scalar(c):
            cw, fc = SIZES[c] * I, T1_VECTOR_COLS[c]
            if fc < cw:
                nc.scalar.activation(out=tbs[c][:, fc:cw], in_=zs[c][:, fc:cw], func=ACT.Copy, scale=col("c11"))

        def basis(c):
            tb, z, w3 = tbs[c], zs[c], w3s[c]
            cw, fc = SIZES[c] * I, T1_VECTOR_COLS[c]
            ts(tb[:, cw:2 * cw], w3[:, 0:cw], col("m2"), c20, ALU.mult, ALU.add)
            nc.vector.scalar_tensor_tensor(out=tb[:, 2 * cw:3 * cw], in0=w3[:, 0:cw], scalar=col("e3"), in1=z[:, 0:cw],
                                           op0=ALU.add, op1=ALU.mult)
            ts(tb[:, 3 * cw:4 * cw], p4s[c][:, 0:cw], col("m4"), col("k4"), ALU.mult, ALU.add)
            nc.vector.scalar_tensor_tensor(out=tb[:, 4 * cw:5 * cw], in0=p5s[c][:, 0:cw], scalar=col("e5"),
                                           in1=z[:, 0:cw], op0=ALU.add, op1=ALU.mult)
            if fc > 0:
                ts(tb[:, 0:fc], z[:, 0:fc], col("c11"))

        def quantise(c):
            cw, nw = SIZES[c] * I, SIZES[c] * P
            cod = work.tile([P, DEG * NW], U32, name="cod", align_bytes=64)
            scl = work.tile([P, DEG * NW], U8, name="scl", align_bytes=64)
            for d0, d1 in ((2, 4), (4, 5), (0, 2)):
                nc.vector.quantize_mx(out=cod[:, d0 * nw:d1 * nw].bitcast(FP8X4), scales=scl[:, d0 * nw:d1 * nw],
                                      in_=tbs[c][:, d0 * cw:d1 * cw])
            cods[c], scls[c] = cod, scl

        def mx(c):
            nw = SIZES[c] * P
            yt = psum.tile([P, NW], F32, name="yt", tag="yt")
            order = (2, 3, 4, 0, 1)
            for n, d in enumerate(order):
                nc.tensor.matmul_mx(
                    out=yt[:, 0:nw],
                    lhsT=ccod[:, d * O:(d + 1) * O].bitcast(FP8X4), lhsT_scale=cscl[:, d * O:(d + 1) * O],
                    rhs=cods[c][:, d * nw:(d + 1) * nw].bitcast(FP8X4), rhs_scale=scls[c][:, d * nw:(d + 1) * nw],
                    start=(n == 0), stop=(n == DEG - 1))
            yt_ps[c] = yt

        def evacuate(c):
            yts = stat.tile([P, NW], F32, name="yts")
            nw = SIZES[c] * P
            nc.scalar.activation(out=yts[:, 0:nw], in_=yt_ps[c][:, 0:nw], func=ACT.Identity, bias=y0[:, 0:1])
            ytss[c] = yts

        def y_transposes(c):
            yst = psum.tile([P, NW], F32, name="yst", tag="yst")
            for j in range(SIZES[c]):
                nc.tensor.transpose(yst[:, j * O:(j + 1) * O], ytss[c][:, j * P:(j + 1) * P], ident[:])
            ysts[c] = yst

        def stats(c):
            st = stat.tile([P, G, 6], F32, name="st")
            mv = stat.tile([P, G, 2], F32, name="mv")
            for j in range(SIZES[c]):
                nc.vector.bn_stats(out=st[:, j, :], in_=ysts[c][:, j * O:(j + 1) * O])
            for j in range(SIZES[c]):
                nc.vector.bn_aggr(out=mv[:, j, :], in_=st[:, j, :])
            mvs[c] = mv

        def rstd_of(c):
            ve = stat.tile([P, G], F32, name="ve")
            g = SIZES[c]
            ts(ve[:, 0:g], mvs[c][:, 0:g, 1], LN_EPS, op0=ALU.add)
            rstd = stat.tile([P, G], F32, name="rstd")
            nc.gpsimd.tensor_tensor(out=rstd[:, 0:g], in0=ve[:, 0:g], in1=mhalf[:, 0:g], op=ALU.pow)
            rstds[c] = rstd

        def centre(c):
            ycg = psum.tile([P, NW], F32, name="ycg", tag="ycg")
            for j in range(SIZES[c]):
                nc.tensor.matmul(out=ycg[:, j * O:(j + 1) * O], lhsT=ytss[c][:, j * P:(j + 1) * P], rhs=ceng[:],
                                 start=True, stop=True)
            ycgs[c] = ycg

        def final(c, j0, j1):
            if j0 == 0:
                osbs[c] = small.tile([P, G * O], F32, name="osb")
            osb = osbs[c]
            for j in range(j0, j1):
                nc.vector.scalar_tensor_tensor(out=osb[:, j * O:(j + 1) * O], in0=ycgs[c][:, j * O:(j + 1) * O],
                                               scalar=rstds[c][:, j:j + 1], in1=b_b[:], op0=ALU.mult, op1=ALU.add)
            if j1 == SIZES[c]:
                nc.sync.dma_start(out=out_v[:, STARTS[c] * O:(STARTS[c] + SIZES[c]) * O], in_=osb[:, 0:SIZES[c] * O])

        craw4 = craw[:].rearrange("p (t o d) -> p t o d", t=4, o=O, d=6)
        c0 = const.tile([P, 4 * O], BF16, name="c0")
        nc.gpsimd.tensor_scalar(out=c0[:].rearrange("p (t o) -> p t o", t=4), in0=craw4[:, :, :, 0],
                                scalar1=1.0, scalar2=1.0, op0=ALU.mult, op1=ALU.mult)
        cg = const.tile([P, DEG * 4 * O], BF16, name="cg", align_bytes=64)
        for d in range(1, DEG + 1):
            sign = {3: col("sg3"), 5: col("sg5")}.get(d, 1.0)
            nc.gpsimd.tensor_scalar(
                out=cg[:, (d - 1) * 4 * O:d * 4 * O].rearrange("p (o t) -> p o t", t=4),
                in0=craw4[:, :, :, d].rearrange("p t o -> p o t"),
                scalar1=sign, scalar2=1.0, op0=ALU.mult, op1=ALU.mult)
        ccod = const.tile([P, DEG * O], U32, name="ccod", align_bytes=64)
        cscl = const.tile([P, DEG * O], U8, name="cscl", align_bytes=64)
        y0 = const.tile([P, 1], F32, name="y0")
        cen = const.tile([P, O], F32, name="cen")
        ceng = const.tile([P, O], F32, name="ceng")

        def coefficient_work():
            nc.vector.quantize_mx(out=ccod[:, 0:4 * O].bitcast(FP8X4), scales=cscl[:, 0:4 * O], in_=cg[:, 0:16 * O])
            nc.vector.quantize_mx(out=ccod[:, 4 * O:5 * O].bitcast(FP8X4), scales=cscl[:, 4 * O:5 * O],
                                  in_=cg[:, 16 * O:20 * O])
            ps0 = psum.tile([P, 64], F32, name="ps0", tag="ycg")
            for t in range(4):
                nc.tensor.matmul(out=ps0[:], lhsT=c0[:, t * O:(t + 1) * O], rhs=ones[:], start=(t == 0),
                                 stop=(t == 3))
            nc.vector.tensor_copy(out=y0[:], in_=ps0[:, 0:1])
            ts(cen[:], ident[:], -1.0 / O, op0=ALU.add)
            nc.vector.tensor_tensor(out=ceng[:], in0=cen[:], in1=g_b[:], op=ALU.mult)

        for c in range(2):
            x_transposes(c)
            sigmoid(c)
        for k in range(NCH + 4):
            if k < NCH:
                square_w3(k)
            if 0 <= k - 2 < NCH:
                evacuate(k - 2)
            if k < NCH:
                squares_p4_p5(k)
            if 1 <= k and k + 1 < NCH:
                x_transposes(k + 1)
            if k + 4 < NCH:
                load_x(k + 4)
            if 0 <= k - 2 < NCH:
                y_transposes(k - 2)
            if 0 <= k - 4:
                centre(k - 4)
            if 0 <= k - 1 < NCH:
                mx(k - 1)
            if 1 <= k and k + 1 < NCH:
                sigmoid(k + 1)
            if k < NCH:
                t1_scalar(k)
                basis(k)
            if k == 0:
                coefficient_work()
            if 0 <= k - 3 < NCH:
                rstd_of(k - 3)
            if 0 <= k - 2 < NCH:
                stats(k - 2)
            if 0 <= k - 4:
                final(k - 4, 0, SIZES[k - 4])
            if k < NCH:
                quantise(k)
